import numpy as np
import ml_dtypes


def mxq(x, axis, fmt="e4m3"):
    dtype, down = {"e4m3": (ml_dtypes.float8_e4m3fn, 7), "e5m2": (ml_dtypes.float8_e5m2, 14)}[fmt]
    v = np.moveaxis(np.asarray(x, np.float32).astype(ml_dtypes.bfloat16).astype(np.float64), axis, -1)
    blocks = v.reshape(v.shape[:-1] + (-1, 32))
    amax = np.abs(blocks).max(-1, keepdims=True)
    byte = np.maximum(np.where(amax > 0, np.frexp(amax)[1] - 1 + 127, 0) - down, 1)
    scale = np.exp2(byte - 127.0)
    codes = (blocks / scale).astype(np.float32).astype(dtype).astype(np.float64)
    return np.moveaxis((codes * scale).reshape(v.shape), -1, axis)


WIDE = False


def mx_kscale(k):
    if not WIDE:
        return np.ones(k)
    levels = np.array([10, -10, 5, -5, 0])
    a = np.random.permutation(np.resize(levels, k // 512 * 4)).reshape(k // 512, 4)
    idx = np.arange(k)
    return np.exp2(a[idx // 512, idx % 128 // 32])


BF16 = ml_dtypes.bfloat16


def bf(x):
    return np.asarray(x, np.float32).astype(BF16)


def f64(x):
    return np.asarray(x).astype(np.float64)


E2M1 = np.array([0.0, 0.5, 1.0, 1.5, 2.0, 3.0, 4.0, 6.0, -0.0, -0.5, -1.0, -1.5, -2.0, -3.0, -4.0, -6.0])


def pack_weight(w, fmt):
    k, n = w.shape
    w = f64(bf(w)).reshape(k // 32, 32, n)
    amax = np.abs(w).max(1)
    if fmt == "e4m3":
        byte = np.frexp(amax)[1] - 1 + 127 - 7
    else:
        mant, ex = np.frexp(amax / 6.0)
        byte = np.where(mant > 0.5, ex, ex - 1) + 127
    byte = np.clip(np.where(amax > 0, byte, 1), 1, 254)
    scaled = (w * np.exp2(127.0 - byte)[:, None, :]).reshape(k, n).astype(np.float32)
    by_word = np.ascontiguousarray(scaled.reshape(k // 512, 128, 4, n).transpose(0, 1, 3, 2))
    if fmt == "e4m3":
        words = by_word.astype(ml_dtypes.float8_e4m3fn).view(np.uint8)
    else:
        c = by_word.astype(ml_dtypes.float4_e2m1fn).view(np.uint8) & 0xF
        words = c[..., 0::2] | (c[..., 1::2] << 4)
    return np.ascontiguousarray(words), np.ascontiguousarray(byte.astype(np.uint8).reshape(k // 512, 16, n))


def unpack_weight(words, scales, fmt):
    g, p, n, _ = words.shape
    if fmt == "e4m3":
        vals = np.ascontiguousarray(words).view(ml_dtypes.float8_e4m3fn).astype(np.float64)
    else:
        nib = np.empty((g, p, n, 4), np.uint8)
        nib[..., 0::2] = words & 0xF
        nib[..., 1::2] = words >> 4
        vals = E2M1[nib]
    vals = vals * np.repeat(np.exp2(scales.astype(np.float64) - 127.0), 8, axis=1)[..., None]
    return vals.transpose(0, 1, 3, 2).reshape(g * 512, n)


B, S, D, DV, NS, SD = 4, 128, 1024, 1024, 4, 256
R = B * S
FMT = "e4m3"


def silu(v):
    return v / (1.0 + np.exp(-v))


def setup_inputs():
    s, r, t = mx_kscale(D), mx_kscale(D), mx_kscale(DV)
    x = bf(np.random.standard_normal((B, S, D)) * r)
    h = bf(np.random.standard_normal((B, S, D)) * s)
    wv = np.random.standard_normal((NS, DV, D)) / np.sqrt(D) * t[:, None] / s
    w1 = np.random.standard_normal((NS, SD, D + DV)) / np.sqrt(D + DV) / np.concatenate([r, t])
    wv_words, wv_scales = pack_weight(wv.swapaxes(1, 2).reshape(-1, DV), FMT)
    w1_words, w1_scales = pack_weight(w1.swapaxes(1, 2).reshape(-1, SD), FMT)
    return {"x": x,
            "h": h,
            "Wv_words": wv_words, "Wv_scales": wv_scales,
            "W1_words": w1_words, "W1_scales": w1_scales}


def reference(x, h, Wv_words, Wv_scales, W1_words, W1_scales):
    xf = f64(x).reshape(R, D)
    hf = f64(h).reshape(R, D)
    wv = unpack_weight(Wv_words, Wv_scales, FMT).reshape(NS, D, DV)
    w1 = unpack_weight(W1_words, W1_scales, FMT).reshape(NS, D + DV, SD)
    views = mxq(hf, 1, "e4m3") @ wv
    a = mxq(xf, 1, "e4m3") @ w1[:, :D, :]
    b = mxq(views, 2, "e4m3") @ w1[:, D:, :]
    return silu(a + b).reshape(NS, B, S, SD)

@@ -1,0 +1,224 @@
+from contextlib import ExitStack
+
+import concourse.mybir as mybir
+from concourse.masks import make_identity
+
+F32 = mybir.dt.float32
+BF16 = mybir.dt.bfloat16
+I32 = mybir.dt.int32
+U32 = mybir.dt.uint32
+U8 = mybir.dt.uint8
+FP8X4 = mybir.dt.float8_e4m3fn_x4
+SILU = mybir.ActivationFunctionType.Silu
+
+P = 128
+PACK = 4
+K_PASS = P * PACK
+SUBNETS = 4
+TOKEN_TILES = 4
+D = 1024
+PASSES = D // K_PASS
+SD = 256
+BANK = 512
+HALVES = D // BANK
+PAIR = 2
+PLANES = 4
+
+FLOPS = 2 * TOKEN_TILES * P * SUBNETS * (D * D + 2 * D * SD)
+
+
+def load_scale_planes(nc, planes, scale_rows):
+    for quadrant in range(4):
+        nc.sync.dma_start(
+            out=planes[32 * quadrant : 32 * quadrant + 4 * PLANES, :].bitcast(I32),
+            in_=scale_rows[:, 4 * quadrant : 4 * quadrant + 4, :].bitcast(I32),
+        )
+
+
+def transpose_and_quantise(nc, banks, work, identity, word_views, codes, scales):
+    grouped = work.tile([P, PAIR, D], BF16, tag="grouped", align_bytes=64)
+    for j in range(PAIR):
+        flipped = banks.tile([P, PASSES, 2, P], F32, tag="bank")
+        for c in range(PASSES):
+            for u in range(2):
+                nc.tensor.transpose(
+                    out=flipped[:, c, u, :], in_=word_views[j][:, c, u, :], identity=identity[:]
+                )
+        side_by_side = grouped[:, j, :].bitcast(F32).rearrange("p (c r u) -> p c r u", c=PASSES, u=2)
+        planes_apart = flipped[:].rearrange("p c u r -> p c r u")
+        if j == 0:
+            nc.vector.tensor_copy(out=side_by_side, in_=planes_apart)
+        else:
+            nc.scalar.copy(out=side_by_side, in_=planes_apart)
+    nc.vector.quantize_mx(
+        out=codes.bitcast(FP8X4),
+        scales=scales,
+        in_=grouped[:].rearrange("p j k -> p (j k)"),
+    )
+
+
+def tile_distributedb_pa_e_kernel(tc, x, h, Wv_words, Wv_scales, W1_words, W1_scales, out):
+    nc = tc.nc
+    with ExitStack() as ctx:
+        keep = ctx.enter_context(tc.tile_pool(name="keep", bufs=1))
+        work = ctx.enter_context(tc.tile_pool(name="work", bufs=4))
+        banks = ctx.enter_context(tc.psum_pool(name="banks", bufs=8))
+        ctx.enter_context(tc.manual_schedule())
+
+        wv_planes = [
+            keep.tile([P, D], U8, name="wv_planes%d" % s, align_bytes=64)
+            for s in range(SUBNETS * PASSES // PLANES)
+        ]
+        w1_planes = [
+            keep.tile([P, SD], U8, name="w1_planes%d" % e, align_bytes=64) for e in range(SUBNETS)
+        ]
+        for planes in wv_planes + w1_planes:
+            nc.vector.memset(planes[:].bitcast(I32), 0)
+        identity = keep.tile([P, P], F32, name="identity")
+        make_identity(nc, identity[:])
+        zero = keep.tile([P, 1], F32, name="zero")
+        nc.vector.memset(zero[:], 0.0)
+        table_warm = keep.tile([P, 1], F32, name="table_warm")
+        nc.scalar.activation(out=table_warm[:], in_=zero[:], func=SILU)
+
+        h_rows = [keep.tile([P, D], BF16, name="h_rows%d" % r) for r in range(TOKEN_TILES)]
+        x_rows = [keep.tile([P, D], BF16, name="x_rows%d" % r) for r in range(TOKEN_TILES)]
+        wv_words = [
+            [keep.tile([P, PASSES, BANK], U32, name="wv_words%d_%d" % (e, half), align_bytes=64)
+             for half in range(HALVES)]
+            for e in range(SUBNETS)
+        ]
+        w1_words = [
+            keep.tile([P, 2 * PASSES, SD], U32, name="w1_words%d" % e, align_bytes=64)
+            for e in range(SUBNETS)
+        ]
+
+        def load_wv(e):
+            if e % 2 == 0:
+                load_scale_planes(nc, wv_planes[e // 2], Wv_scales[2 * e : 2 * e + PLANES])
+            for half in range(HALVES):
+                columns = slice(half * BANK, (half + 1) * BANK)
+                nc.sync.dma_start(
+                    out=wv_words[e][half][:].bitcast(I32),
+                    in_=Wv_words[PASSES * e : PASSES * (e + 1), :, columns, :]
+                    .rearrange("c p n t -> p c (n t)")
+                    .bitcast(I32),
+                )
+
+        def load_w1(e):
+            groups = slice(2 * PASSES * e, 2 * PASSES * (e + 1))
+            load_scale_planes(nc, w1_planes[e], W1_scales[groups])
+            nc.sync.dma_start(
+                out=w1_words[e][:].bitcast(I32),
+                in_=W1_words[groups].rearrange("g p n t -> p g (n t)").bitcast(I32),
+            )
+
+        for r in range(TOKEN_TILES):
+            nc.sync.dma_start(out=h_rows[r][:], in_=h[r])
+        load_wv(0)
+        for r in range(TOKEN_TILES):
+            nc.sync.dma_start(out=x_rows[r][:], in_=x[r])
+        load_w1(0)
+        for e in range(1, SUBNETS):
+            load_wv(e)
+            load_w1(e)
+
+        h_codes = keep.tile([P, TOKEN_TILES, PASSES, P], U32, name="h_codes", align_bytes=64)
+        h_scales = keep.tile([P, TOKEN_TILES, PASSES, P], U8, name="h_scales", align_bytes=64)
+        x_codes = keep.tile([P, TOKEN_TILES, PASSES, P], U32, name="x_codes", align_bytes=64)
+        x_scales = keep.tile([P, TOKEN_TILES, PASSES, P], U8, name="x_scales", align_bytes=64)
+
+        def quantise_input(rows, codes, scales, pair):
+            tiles = slice(PAIR * pair, PAIR * (pair + 1))
+            transpose_and_quantise(
+                nc, banks, work, identity,
+                [rows[PAIR * pair + j][:].bitcast(F32).rearrange("r (c p u) -> r c u p", c=PASSES, u=2)
+                 for j in range(PAIR)],
+                codes[:, tiles].rearrange("p r c t -> p (r c t)"),
+                scales[:, tiles].rearrange("p r c t -> p (r c t)"),
+            )
+
+        rounds = [(e, pair) for e in range(SUBNETS) for pair in range(TOKEN_TILES // PAIR)]
+        views_rows = {}
+        views_mx = {}
+
+        def stage1(i):
+            e, pair = rounds[i]
+            views_rows[i] = [
+                work.tile([P, D], BF16, name="views_rows", tag="views_rows", bufs=3 * PAIR)
+                for j in range(PAIR)
+            ]
+            for half in range(HALVES):
+                for j in range(PAIR):
+                    r = PAIR * pair + j
+                    acc = banks.tile([P, BANK], F32, tag="bank")
+                    for c in range(PASSES):
+                        group = PASSES * e + c
+                        nc.tensor.matmul_mx(
+                            out=acc[:],
+                            lhsT=h_codes[:, r, c, :].bitcast(FP8X4),
+                            lhsT_scale=h_scales[:, r, c, :],
+                            rhs=wv_words[e][half][:, c, :].bitcast(FP8X4),
+                            rhs_scale=wv_planes[group // PLANES][
+                                4 * (group % PLANES) : P, half * BANK : (half + 1) * BANK
+                            ],
+                            start=(c == 0),
+                            stop=(c == PASSES - 1),
+                        )
+                    sorted_words = views_rows[i][j][:, half * BANK : (half + 1) * BANK].rearrange(
+                        "r (u p s) -> r u p s", u=2, s=2
+                    )
+                    in_feature_order = acc[:].rearrange("r (p u s) -> r u p s", u=2, s=2)
+                    if j == 0:
+                        nc.vector.tensor_copy(out=sorted_words, in_=in_feature_order)
+                    else:
+                        nc.scalar.copy(out=sorted_words, in_=in_feature_order)
+
+        def quantise_views(i):
+            codes = work.tile([P, PAIR, PASSES, P], U32, tag="views_codes", align_bytes=64)
+            scales = work.tile([P, PAIR, PASSES, P], U8, tag="views_scales", align_bytes=64)
+            views_mx[i] = (codes, scales)
+            transpose_and_quantise(
+                nc, banks, work, identity,
+                [views_rows[i][j][:].bitcast(F32).rearrange("r (c u p) -> r c u p", c=PASSES, u=2)
+                 for j in range(PAIR)],
+                codes[:].rearrange("p r c t -> p (r c t)"),
+                scales[:].rearrange("p r c t -> p (r c t)"),
+            )
+
+        def stage2(i):
+            e, pair = rounds[i]
+            codes, scales = views_mx[i]
+            acc = banks.tile([P, PAIR, SD], F32, tag="bank")
+            for j in range(PAIR):
+                r = PAIR * pair + j
+                operands = [(x_codes[:, r, c, :], x_scales[:, r, c, :]) for c in range(PASSES)]
+                operands += [(codes[:, j, c, :], scales[:, j, c, :]) for c in range(PASSES)]
+                for g in range(2 * PASSES):
+                    nc.tensor.matmul_mx(
+                        out=acc[:, j, :],
+                        lhsT=operands[g][0].bitcast(FP8X4),
+                        lhsT_scale=operands[g][1],
+                        rhs=w1_words[e][:, g, :].bitcast(FP8X4),
+                        rhs_scale=w1_planes[e][4 * g : P, :],
+                        start=(g == 0),
+                        stop=(g == 2 * PASSES - 1),
+                    )
+            mid = work.tile([P, PAIR, SD], F32, tag="mid")
+            nc.scalar.activation(out=mid[:], in_=acc[:], func=SILU)
+            nc.sync.dma_start(
+                out=out[e, PAIR * pair : PAIR * (pair + 1)].rearrange("b s f -> s b f"), in_=mid[:]
+            )
+
+        for pair in range(TOKEN_TILES // PAIR):
+            quantise_input(h_rows, h_codes, h_scales, pair)
+        for i in range(len(rounds) + 2):
+            if i < len(rounds):
+                stage1(i)
+            if i == 0:
+                for pair in range(TOKEN_TILES // PAIR):
+                    quantise_input(x_rows, x_codes, x_scales, pair)
+            if 1 <= i <= len(rounds):
+                quantise_views(i - 1)
+            if i >= 2:
+                stage2(i - 2)

@@ -22,6 +22,7 @@ SD = 256
 BANK = 512
 HALVES = D // BANK
 PAIR = 2
+PAIRS = TOKEN_TILES // PAIR
 PLANES = 4
 
 FLOPS = 2 * TOKEN_TILES * P * SUBNETS * (D * D + 2 * D * SD)
@@ -116,41 +117,55 @@ def tile_distributedb_pa_e_kernel(tc, x, h, Wv_words, Wv_scales, W1_words, W1_sc
         for r in range(TOKEN_TILES):
             nc.sync.dma_start(out=h_rows[r][:], in_=h[r])
         load_wv(0)
+        load_wv(1)
         for r in range(TOKEN_TILES):
             nc.sync.dma_start(out=x_rows[r][:], in_=x[r])
-        load_w1(0)
-        for e in range(1, SUBNETS):
-            load_wv(e)
+        for e in range(SUBNETS):
             load_w1(e)
+            if e + 2 < SUBNETS:
+                load_wv(e + 2)
 
         h_codes = keep.tile([P, TOKEN_TILES, PASSES, P], U32, name="h_codes", align_bytes=64)
         h_scales = keep.tile([P, TOKEN_TILES, PASSES, P], U8, name="h_scales", align_bytes=64)
         x_codes = keep.tile([P, TOKEN_TILES, PASSES, P], U32, name="x_codes", align_bytes=64)
         x_scales = keep.tile([P, TOKEN_TILES, PASSES, P], U8, name="x_scales", align_bytes=64)
+        x_sorted = [keep.tile([P, D], BF16, name="x_sorted%d" % r) for r in range(TOKEN_TILES)]
 
-        def quantise_input(rows, codes, scales, pair):
-            tiles = slice(PAIR * pair, PAIR * (pair + 1))
-            transpose_and_quantise(
-                nc, banks, work, identity,
-                [rows[PAIR * pair + j][:].bitcast(F32).rearrange("r (c p u) -> r c u p", c=PASSES, u=2)
-                 for j in range(PAIR)],
-                codes[:, tiles].rearrange("p r c t -> p (r c t)"),
-                scales[:, tiles].rearrange("p r c t -> p (r c t)"),
-            )
+        def copy_on(r, dst, src):
+            if r % 2 == 0:
+                nc.vector.tensor_copy(out=dst, in_=src)
+            else:
+                nc.scalar.copy(out=dst, in_=src)
 
-        rounds = [(e, pair) for e in range(SUBNETS) for pair in range(TOKEN_TILES // PAIR)]
+        def words_in_feature_order(rows):
+            return rows[:].bitcast(F32).rearrange("r (c p u) -> r c u p", c=PASSES, u=2)
+
+        def words_sorted(rows):
+            return rows[:].bitcast(F32).rearrange("r (c u p) -> r c u p", c=PASSES, u=2)
+
+        def quantise_tiles(word_views, codes, scales):
+            for pair in range(PAIRS):
+                tiles = slice(PAIR * pair, PAIR * (pair + 1))
+                transpose_and_quantise(
+                    nc, banks, work, identity, word_views[tiles],
+                    codes[:, tiles].rearrange("p r c t -> p (r c t)"),
+                    scales[:, tiles].rearrange("p r c t -> p (r c t)"),
+                )
+
+        def sort_x():
+            for r in range(TOKEN_TILES):
+                copy_on(r, words_sorted(x_sorted[r]), words_in_feature_order(x_rows[r]))
+
         views_rows = {}
         views_mx = {}
 
-        def stage1(i):
-            e, pair = rounds[i]
-            views_rows[i] = [
-                work.tile([P, D], BF16, name="views_rows", tag="views_rows", bufs=3 * PAIR)
-                for j in range(PAIR)
+        def stage1(e):
+            views_rows[e] = [
+                work.tile([P, D], BF16, name="views_rows", tag="views_rows", bufs=2 * TOKEN_TILES)
+                for r in range(TOKEN_TILES)
             ]
             for half in range(HALVES):
-                for j in range(PAIR):
-                    r = PAIR * pair + j
+                for r in range(TOKEN_TILES):
                     acc = banks.tile([P, BANK], F32, tag="bank")
                     for c in range(PASSES):
                         group = PASSES * e + c
@@ -165,38 +180,29 @@ def tile_distributedb_pa_e_kernel(tc, x, h, Wv_words, Wv_scales, W1_words, W1_sc
                             start=(c == 0),
                             stop=(c == PASSES - 1),
                         )
-                    sorted_words = views_rows[i][j][:, half * BANK : (half + 1) * BANK].rearrange(
-                        "r (u p s) -> r u p s", u=2, s=2
+                    copy_on(
+                        r,
+                        views_rows[e][r][:, half * BANK : (half + 1) * BANK].rearrange(
+                            "r (u p s) -> r u p s", u=2, s=2
+                        ),
+                        acc[:].rearrange("r (p u s) -> r u p s", u=2, s=2),
                     )
-                    in_feature_order = acc[:].rearrange("r (p u s) -> r u p s", u=2, s=2)
-                    if j == 0:
-                        nc.vector.tensor_copy(out=sorted_words, in_=in_feature_order)
-                    else:
-                        nc.scalar.copy(out=sorted_words, in_=in_feature_order)
 
-        def quantise_views(i):
-            codes = work.tile([P, PAIR, PASSES, P], U32, tag="views_codes", align_bytes=64)
-            scales = work.tile([P, PAIR, PASSES, P], U8, tag="views_scales", align_bytes=64)
-            views_mx[i] = (codes, scales)
-            transpose_and_quantise(
-                nc, banks, work, identity,
-                [views_rows[i][j][:].bitcast(F32).rearrange("r (c u p) -> r c u p", c=PASSES, u=2)
-                 for j in range(PAIR)],
-                codes[:].rearrange("p r c t -> p (r c t)"),
-                scales[:].rearrange("p r c t -> p (r c t)"),
-            )
+        def quantise_views(e):
+            codes = work.tile([P, TOKEN_TILES, PASSES, P], U32, tag="views_codes", align_bytes=64)
+            scales = work.tile([P, TOKEN_TILES, PASSES, P], U8, tag="views_scales", align_bytes=64)
+            views_mx[e] = (codes, scales)
+            quantise_tiles([words_sorted(rows) for rows in views_rows[e]], codes, scales)
 
-        def stage2(i):
-            e, pair = rounds[i]
-            codes, scales = views_mx[i]
-            acc = banks.tile([P, PAIR, SD], F32, tag="bank")
-            for j in range(PAIR):
-                r = PAIR * pair + j
+        def stage2(e):
+            codes, scales = views_mx[e]
+            for r in range(TOKEN_TILES):
                 operands = [(x_codes[:, r, c, :], x_scales[:, r, c, :]) for c in range(PASSES)]
-                operands += [(codes[:, j, c, :], scales[:, j, c, :]) for c in range(PASSES)]
+                operands += [(codes[:, r, c, :], scales[:, r, c, :]) for c in range(PASSES)]
+                acc = banks.tile([P, SD], F32, tag="bank")
                 for g in range(2 * PASSES):
                     nc.tensor.matmul_mx(
-                        out=acc[:, j, :],
+                        out=acc[:],
                         lhsT=operands[g][0].bitcast(FP8X4),
                         lhsT_scale=operands[g][1],
                         rhs=w1_words[e][:, g, :].bitcast(FP8X4),
@@ -204,21 +210,19 @@ def tile_distributedb_pa_e_kernel(tc, x, h, Wv_words, Wv_scales, W1_words, W1_sc
                         start=(g == 0),
                         stop=(g == 2 * PASSES - 1),
                     )
-            mid = work.tile([P, PAIR, SD], F32, tag="mid")
-            nc.scalar.activation(out=mid[:], in_=acc[:], func=SILU)
-            nc.sync.dma_start(
-                out=out[e, PAIR * pair : PAIR * (pair + 1)].rearrange("b s f -> s b f"), in_=mid[:]
-            )
+                mid = work.tile([P, SD], F32, tag="mid")
+                nc.scalar.activation(out=mid[:], in_=acc[:], func=SILU)
+                nc.sync.dma_start(out=out[e, r], in_=mid[:])
 
-        for pair in range(TOKEN_TILES // PAIR):
-            quantise_input(h_rows, h_codes, h_scales, pair)
-        for i in range(len(rounds) + 2):
-            if i < len(rounds):
+        quantise_tiles([words_in_feature_order(rows) for rows in h_rows], h_codes, h_scales)
+        for i in range(SUBNETS + 2):
+            if i < SUBNETS:
                 stage1(i)
-            if i == 0:
-                for pair in range(TOKEN_TILES // PAIR):
-                    quantise_input(x_rows, x_codes, x_scales, pair)
-            if 1 <= i <= len(rounds):
+            if i == 2:
+                quantise_tiles([words_sorted(rows) for rows in x_sorted], x_codes, x_scales)
+            if 1 <= i <= SUBNETS:
                 quantise_views(i - 1)
+            if i == 1:
+                sort_x()
             if i >= 2:
                 stage2(i - 2)

@@ -106,24 +106,23 @@ def tile_distributedb_pa_e_kernel(tc, x, h, Wv_words, Wv_scales, W1_words, W1_sc
                     .bitcast(I32),
                 )
 
-        def load_w1(e):
-            groups = slice(2 * PASSES * e, 2 * PASSES * (e + 1))
-            load_scale_planes(nc, w1_planes[e], W1_scales[groups])
-            nc.sync.dma_start(
-                out=w1_words[e][:].bitcast(I32),
-                in_=W1_words[groups].rearrange("g p n t -> p g (n t)").bitcast(I32),
-            )
+        def w1_groups(e):
+            return slice(2 * PASSES * e, 2 * PASSES * (e + 1))
 
         for r in range(TOKEN_TILES):
             nc.sync.dma_start(out=h_rows[r][:], in_=h[r])
-        load_wv(0)
-        load_wv(1)
+        for e in range(SUBNETS - 1):
+            load_wv(e)
         for r in range(TOKEN_TILES):
             nc.sync.dma_start(out=x_rows[r][:], in_=x[r])
+        load_wv(SUBNETS - 1)
         for e in range(SUBNETS):
-            load_w1(e)
-            if e + 2 < SUBNETS:
-                load_wv(e + 2)
+            load_scale_planes(nc, w1_planes[e], W1_scales[w1_groups(e)])
+        for e in range(SUBNETS):
+            nc.sync.dma_start(
+                out=w1_words[e][:].bitcast(I32),
+                in_=W1_words[w1_groups(e)].rearrange("g p n t -> p g (n t)").bitcast(I32),
+            )
 
         h_codes = keep.tile([P, TOKEN_TILES, PASSES, P], U32, name="h_codes", align_bytes=64)
         h_scales = keep.tile([P, TOKEN_TILES, PASSES, P], U8, name="h_scales", align_bytes=64)

@@ -16,14 +16,16 @@ PACK = 4
 K_PASS = P * PACK
 SUBNETS = 4
 TOKEN_TILES = 4
+UNITS = SUBNETS * TOKEN_TILES
 D = 1024
 PASSES = D // K_PASS
 SD = 256
-BANK = 512
-HALVES = D // BANK
 PAIR = 2
 PAIRS = TOKEN_TILES // PAIR
 PLANES = 4
+STEPS = SUBNETS * PASSES * TOKEN_TILES
+STAGE2_DELAY = 10
+VECTOR_BANK = 2
 
 FLOPS = 2 * TOKEN_TILES * P * SUBNETS * (D * D + 2 * D * SD)
 
@@ -36,7 +38,7 @@ def load_scale_planes(nc, planes, scale_rows):
         )
 
 
-def transpose_and_quantise(nc, banks, work, identity, word_views, codes, scales):
+def transpose_and_quantise(nc, banks, work, identity, word_views, codes, scales, vector_helps):
     grouped = work.tile([P, PAIR, D], BF16, tag="grouped", align_bytes=64)
     for j in range(PAIR):
         flipped = banks.tile([P, PASSES, 2, P], F32, tag="bank")
@@ -47,7 +49,7 @@ def transpose_and_quantise(nc, banks, work, identity, word_views, codes, scales)
                 )
         side_by_side = grouped[:, j, :].bitcast(F32).rearrange("p (c r u) -> p c r u", c=PASSES, u=2)
         planes_apart = flipped[:].rearrange("p c u r -> p c r u")
-        if j == 0:
+        if j == 0 and vector_helps:
             nc.vector.tensor_copy(out=side_by_side, in_=planes_apart)
         else:
             nc.scalar.copy(out=side_by_side, in_=planes_apart)
@@ -66,6 +68,10 @@ def tile_distributedb_pa_e_kernel(tc, x, h, Wv_words, Wv_scales, W1_words, W1_sc
         banks = ctx.enter_context(tc.psum_pool(name="banks", bufs=8))
         ctx.enter_context(tc.manual_schedule())
 
+        wv_planes_loaded = [
+            keep.tile([P, D], U8, name="wv_planes_loaded%d" % s, align_bytes=64)
+            for s in range(SUBNETS * PASSES // PLANES)
+        ]
         wv_planes = [
             keep.tile([P, D], U8, name="wv_planes%d" % s, align_bytes=64)
             for s in range(SUBNETS * PASSES // PLANES)
@@ -73,7 +79,7 @@ def tile_distributedb_pa_e_kernel(tc, x, h, Wv_words, Wv_scales, W1_words, W1_sc
         w1_planes = [
             keep.tile([P, SD], U8, name="w1_planes%d" % e, align_bytes=64) for e in range(SUBNETS)
         ]
-        for planes in wv_planes + w1_planes:
+        for planes in wv_planes_loaded + w1_planes:
             nc.vector.memset(planes[:].bitcast(I32), 0)
         identity = keep.tile([P, P], F32, name="identity")
         make_identity(nc, identity[:])
@@ -84,9 +90,14 @@ def tile_distributedb_pa_e_kernel(tc, x, h, Wv_words, Wv_scales, W1_words, W1_sc
 
         h_rows = [keep.tile([P, D], BF16, name="h_rows%d" % r) for r in range(TOKEN_TILES)]
         x_rows = [keep.tile([P, D], BF16, name="x_rows%d" % r) for r in range(TOKEN_TILES)]
-        wv_words = [
-            [keep.tile([P, PASSES, BANK], U32, name="wv_words%d_%d" % (e, half), align_bytes=64)
-             for half in range(HALVES)]
+        wv_loaded = [
+            [keep.tile([P, PASSES, K_PASS], U32, name="wv_loaded%d_%d" % (e, a), align_bytes=64)
+             for a in range(PASSES)]
+            for e in range(SUBNETS)
+        ]
+        wv_sorted = [
+            [keep.tile([P, PASSES, K_PASS], U32, name="wv_sorted%d_%d" % (e, a), align_bytes=64)
+             for a in range(PASSES)]
             for e in range(SUBNETS)
         ]
         w1_words = [
@@ -94,35 +105,47 @@ def tile_distributedb_pa_e_kernel(tc, x, h, Wv_words, Wv_scales, W1_words, W1_sc
             for e in range(SUBNETS)
         ]
 
-        def load_wv(e):
-            if e % 2 == 0:
-                load_scale_planes(nc, wv_planes[e // 2], Wv_scales[2 * e : 2 * e + PLANES])
-            for half in range(HALVES):
-                columns = slice(half * BANK, (half + 1) * BANK)
-                nc.sync.dma_start(
-                    out=wv_words[e][half][:].bitcast(I32),
-                    in_=Wv_words[PASSES * e : PASSES * (e + 1), :, columns, :]
-                    .rearrange("c p n t -> p c (n t)")
-                    .bitcast(I32),
-                )
+        def load_wv(e, a):
+            columns = slice(a * K_PASS, (a + 1) * K_PASS)
+            nc.sync.dma_start(
+                out=wv_loaded[e][a][:].bitcast(I32),
+                in_=Wv_words[PASSES * e : PASSES * (e + 1), :, columns, :]
+                .rearrange("c p n t -> p c (n t)")
+                .bitcast(I32),
+            )
 
         def w1_groups(e):
             return slice(2 * PASSES * e, 2 * PASSES * (e + 1))
 
-        for r in range(TOKEN_TILES):
-            nc.sync.dma_start(out=h_rows[r][:], in_=h[r])
-        for e in range(SUBNETS - 1):
-            load_wv(e)
-        for r in range(TOKEN_TILES):
-            nc.sync.dma_start(out=x_rows[r][:], in_=x[r])
-        load_wv(SUBNETS - 1)
-        for e in range(SUBNETS):
-            load_scale_planes(nc, w1_planes[e], W1_scales[w1_groups(e)])
-        for e in range(SUBNETS):
+        def load_w1(e):
             nc.sync.dma_start(
                 out=w1_words[e][:].bitcast(I32),
                 in_=W1_words[w1_groups(e)].rearrange("g p n t -> p g (n t)").bitcast(I32),
             )
+
+        def load_wv_planes(s):
+            load_scale_planes(nc, wv_planes_loaded[s], Wv_scales[PLANES * s : PLANES * (s + 1)])
+
+        load_wv_planes(0)
+        for r in range(TOKEN_TILES):
+            nc.sync.dma_start(out=h_rows[r][:], in_=h[r])
+        load_wv(0, 0)
+        load_wv(0, 1)
+        for r in range(TOKEN_TILES):
+            nc.sync.dma_start(out=x_rows[r][:], in_=x[r])
+        load_wv(1, 0)
+        for e in range(SUBNETS):
+            load_scale_planes(nc, w1_planes[e], W1_scales[w1_groups(e)])
+        load_w1(0)
+        load_wv(1, 1)
+        load_w1(1)
+        load_wv_planes(1)
+        load_wv(2, 0)
+        load_wv(2, 1)
+        load_w1(2)
+        load_wv(3, 0)
+        load_wv(3, 1)
+        load_w1(3)
 
         h_codes = keep.tile([P, TOKEN_TILES, PASSES, P], U32, name="h_codes", align_bytes=64)
         h_scales = keep.tile([P, TOKEN_TILES, PASSES, P], U8, name="h_scales", align_bytes=64)
@@ -130,98 +153,143 @@ def tile_distributedb_pa_e_kernel(tc, x, h, Wv_words, Wv_scales, W1_words, W1_sc
         x_scales = keep.tile([P, TOKEN_TILES, PASSES, P], U8, name="x_scales", align_bytes=64)
         x_sorted = [keep.tile([P, D], BF16, name="x_sorted%d" % r) for r in range(TOKEN_TILES)]
 
-        def copy_on(r, dst, src):
-            if r % 2 == 0:
-                nc.vector.tensor_copy(out=dst, in_=src)
-            else:
-                nc.scalar.copy(out=dst, in_=src)
-
         def words_in_feature_order(rows):
             return rows[:].bitcast(F32).rearrange("r (c p u) -> r c u p", c=PASSES, u=2)
 
         def words_sorted(rows):
             return rows[:].bitcast(F32).rearrange("r (c u p) -> r c u p", c=PASSES, u=2)
 
-        def quantise_tiles(word_views, codes, scales):
+        def quantise_tiles(word_views, codes, scales, vector_helps):
             for pair in range(PAIRS):
                 tiles = slice(PAIR * pair, PAIR * (pair + 1))
                 transpose_and_quantise(
                     nc, banks, work, identity, word_views[tiles],
                     codes[:, tiles].rearrange("p r c t -> p (r c t)"),
                     scales[:, tiles].rearrange("p r c t -> p (r c t)"),
+                    vector_helps,
                 )
 
         def sort_x():
             for r in range(TOKEN_TILES):
-                copy_on(r, words_sorted(x_sorted[r]), words_in_feature_order(x_rows[r]))
+                nc.vector.tensor_copy(out=words_sorted(x_sorted[r]), in_=words_in_feature_order(x_rows[r]))
 
-        views_rows = {}
+        def sort_wv_planes(s, a):
+            columns = slice(a * K_PASS, (a + 1) * K_PASS)
+            nc.vector.tensor_copy(
+                out=wv_planes[s][:, columns].rearrange("p (t m) -> p t m", t=PACK),
+                in_=wv_planes_loaded[s][:, columns].rearrange("p (m t) -> p t m", t=PACK),
+            )
+
+        def sort_wv(e, a, t_from, t_to):
+            nc.vector.tensor_copy(
+                out=wv_sorted[e][a][:].bitcast(I32).rearrange("p c (t m) -> p c t m", t=PACK)[:, :, t_from:t_to, :],
+                in_=wv_loaded[e][a][:].bitcast(I32).rearrange("p c (m t) -> p c t m", t=PACK)[:, :, t_from:t_to, :],
+            )
+
+        views_banks = {}
+        views_grouped = {}
         views_mx = {}
 
-        def stage1(e):
-            views_rows[e] = [
-                work.tile([P, D], BF16, name="views_rows", tag="views_rows", bufs=2 * TOKEN_TILES)
-                for r in range(TOKEN_TILES)
-            ]
-            for half in range(HALVES):
+        def open_bank(e, a, r):
+            acc = banks.tile([P, PACK, P], F32, tag="bank")
+            views_banks[(e, a, r)] = acc
+
+        def stage1_passes(e, a, r, t):
+            for c in range(PASSES):
+                group = PASSES * e + c
+                nc.tensor.matmul_mx(
+                    out=views_banks[(e, a, r)][:, t, :],
+                    lhsT=wv_sorted[e][a][:, c, t * P : (t + 1) * P].bitcast(FP8X4),
+                    lhsT_scale=wv_planes[group // PLANES][
+                        4 * (group % PLANES) : P, a * K_PASS + t * P : a * K_PASS + (t + 1) * P
+                    ],
+                    rhs=h_codes[:, r, c, :].bitcast(FP8X4),
+                    rhs_scale=h_scales[:, r, c, :],
+                    start=(c == 0),
+                    stop=(c == PASSES - 1),
+                )
+
+        def round_views(e, a, r):
+            unit = TOKEN_TILES * e + r
+            if a == 0:
+                grouped = work.tile([P, PASSES, P, PACK], BF16, tag="views_grouped", align_bytes=64, bufs=8)
+                views_grouped[unit] = grouped
+            four_apart = views_banks[(e, a, r)][:].rearrange("p t n -> p n t")
+            if r == VECTOR_BANK:
+                nc.vector.tensor_copy(out=views_grouped[unit][:, a, :, :], in_=four_apart)
+            else:
+                nc.scalar.copy(out=views_grouped[unit][:, a, :, :], in_=four_apart)
+
+        def quantise_views(unit):
+            codes = work.tile([P, PASSES, P], U32, tag="views_codes", align_bytes=64, bufs=8)
+            scales = work.tile([P, PASSES, P], U8, tag="views_scales", align_bytes=64, bufs=8)
+            views_mx[unit] = (codes, scales)
+            nc.vector.quantize_mx(
+                out=codes[:].rearrange("p a n -> p (a n)").bitcast(FP8X4),
+                scales=scales[:].rearrange("p a n -> p (a n)"),
+                in_=views_grouped[unit][:].rearrange("p a n t -> p (a n t)"),
+            )
+
+        def stage2(unit):
+            e, r = divmod(unit, TOKEN_TILES)
+            codes, scales = views_mx[unit]
+            operands = [(x_codes[:, r, c, :], x_scales[:, r, c, :]) for c in range(PASSES)]
+            operands += [(codes[:, a, :], scales[:, a, :]) for a in range(PASSES)]
+            acc = banks.tile([P, SD], F32, tag="bank")
+            for g in range(2 * PASSES):
+                nc.tensor.matmul_mx(
+                    out=acc[:],
+                    lhsT=operands[g][0].bitcast(FP8X4),
+                    lhsT_scale=operands[g][1],
+                    rhs=w1_words[e][:, g, :].bitcast(FP8X4),
+                    rhs_scale=w1_planes[e][4 * g : P, :],
+                    start=(g == 0),
+                    stop=(g == 2 * PASSES - 1),
+                )
+            mid = work.tile([P, SD], F32, tag="mid")
+            nc.scalar.activation(out=mid[:], in_=acc[:], func=SILU)
+            nc.sync.dma_start(out=out[e, r], in_=mid[:])
+
+        def split(j):
+            phase, r = divmod(j, TOKEN_TILES)
+            e, a = divmod(phase, PASSES)
+            return e, a, r
+
+        stage2_after = {}
+        for unit in range(UNITS):
+            e, r = divmod(unit, TOKEN_TILES)
+            stage2_after.setdefault(min(2 * TOKEN_TILES * e + STAGE2_DELAY + 2 * r, STEPS), []).append(unit)
+
+        sort_wv_planes(0, 0)
+        quantise_tiles([words_in_feature_order(rows) for rows in h_rows], h_codes, h_scales, False)
+        for j in range(STEPS + 1):
+            if j == 0:
                 for r in range(TOKEN_TILES):
-                    acc = banks.tile([P, BANK], F32, tag="bank")
-                    for c in range(PASSES):
-                        group = PASSES * e + c
-                        nc.tensor.matmul_mx(
-                            out=acc[:],
-                            lhsT=h_codes[:, r, c, :].bitcast(FP8X4),
-                            lhsT_scale=h_scales[:, r, c, :],
-                            rhs=wv_words[e][half][:, c, :].bitcast(FP8X4),
-                            rhs_scale=wv_planes[group // PLANES][
-                                4 * (group % PLANES) : P, half * BANK : (half + 1) * BANK
-                            ],
-                            start=(c == 0),
-                            stop=(c == PASSES - 1),
-                        )
-                    copy_on(
-                        r,
-                        views_rows[e][r][:, half * BANK : (half + 1) * BANK].rearrange(
-                            "r (u p s) -> r u p s", u=2, s=2
-                        ),
-                        acc[:].rearrange("r (p u s) -> r u p s", u=2, s=2),
-                    )
-
-        def quantise_views(e):
-            codes = work.tile([P, TOKEN_TILES, PASSES, P], U32, tag="views_codes", align_bytes=64)
-            scales = work.tile([P, TOKEN_TILES, PASSES, P], U8, tag="views_scales", align_bytes=64)
-            views_mx[e] = (codes, scales)
-            quantise_tiles([words_sorted(rows) for rows in views_rows[e]], codes, scales)
-
-        def stage2(e):
-            codes, scales = views_mx[e]
-            for r in range(TOKEN_TILES):
-                operands = [(x_codes[:, r, c, :], x_scales[:, r, c, :]) for c in range(PASSES)]
-                operands += [(codes[:, r, c, :], scales[:, r, c, :]) for c in range(PASSES)]
-                acc = banks.tile([P, SD], F32, tag="bank")
-                for g in range(2 * PASSES):
-                    nc.tensor.matmul_mx(
-                        out=acc[:],
-                        lhsT=operands[g][0].bitcast(FP8X4),
-                        lhsT_scale=operands[g][1],
-                        rhs=w1_words[e][:, g, :].bitcast(FP8X4),
-                        rhs_scale=w1_planes[e][4 * g : P, :],
-                        start=(g == 0),
-                        stop=(g == 2 * PASSES - 1),
-                    )
-                mid = work.tile([P, SD], F32, tag="mid")
-                nc.scalar.activation(out=mid[:], in_=acc[:], func=SILU)
-                nc.sync.dma_start(out=out[e, r], in_=mid[:])
-
-        quantise_tiles([words_in_feature_order(rows) for rows in h_rows], h_codes, h_scales)
-        for i in range(SUBNETS + 2):
-            if i < SUBNETS:
-                stage1(i)
-            if i == 2:
-                quantise_tiles([words_sorted(rows) for rows in x_sorted], x_codes, x_scales)
-            if 1 <= i <= SUBNETS:
-                quantise_views(i - 1)
-            if i == 1:
+                    open_bank(0, 0, r)
+                for t in range(PACK):
+                    sort_wv(0, 0, t, t + 1)
+                    for r in range(TOKEN_TILES):
+                        stage1_passes(0, 0, r, t)
+                sort_wv_planes(0, 1)
+            if j < STEPS:
+                e, a, r = split(j)
+                if j >= TOKEN_TILES:
+                    open_bank(e, a, r)
+                    for t in range(PACK):
+                        stage1_passes(e, a, r, t)
+                round_views(e, a, r)
+            if j >= 1:
+                e_done, a_done, r_done = split(j - 1)
+                if a_done == PASSES - 1:
+                    quantise_views(TOKEN_TILES * e_done + r_done)
+            if j == TOKEN_TILES:
                 sort_x()
-            if i >= 2:
-                stage2(i - 2)
+            if j % TOKEN_TILES == 1 and j + 3 < STEPS:
+                e_next, a_next, r_next = split(j + 3)
+                sort_wv(e_next, a_next, 0, PACK)
+            if j == 12 or j == 13:
+                sort_wv_planes(1, j - 12)
+            if j == 2 * TOKEN_TILES - 1:
+                quantise_tiles([words_sorted(rows) for rows in x_sorted], x_codes, x_scales, True)
+            for unit in stage2_after.get(j, []):
+                stage2(unit)

@@ -24,8 +24,9 @@ PAIR = 2
 PAIRS = TOKEN_TILES // PAIR
 PLANES = 4
 STEPS = SUBNETS * PASSES * TOKEN_TILES
-STAGE2_DELAY = 10
-VECTOR_BANK = 2
+STAGE2_DELAY = 5
+X_READY = 10
+VECTOR_BANK = 0
 
 FLOPS = 2 * TOKEN_TILES * P * SUBNETS * (D * D + 2 * D * SD)
 
@@ -38,7 +39,7 @@ def load_scale_planes(nc, planes, scale_rows):
         )
 
 
-def transpose_and_quantise(nc, banks, work, identity, word_views, codes, scales, vector_helps):
+def transpose_pair(nc, banks, work, identity, word_views, vector_helps):
     grouped = work.tile([P, PAIR, D], BF16, tag="grouped", align_bytes=64)
     for j in range(PAIR):
         flipped = banks.tile([P, PASSES, 2, P], F32, tag="bank")
@@ -53,11 +54,7 @@ def transpose_and_quantise(nc, banks, work, identity, word_views, codes, scales,
             nc.vector.tensor_copy(out=side_by_side, in_=planes_apart)
         else:
             nc.scalar.copy(out=side_by_side, in_=planes_apart)
-    nc.vector.quantize_mx(
-        out=codes.bitcast(FP8X4),
-        scales=scales,
-        in_=grouped[:].rearrange("p j k -> p (j k)"),
-    )
+    return grouped
 
 
 def tile_distributedb_pa_e_kernel(tc, x, h, Wv_words, Wv_scales, W1_words, W1_scales, out):
@@ -126,52 +123,52 @@ def tile_distributedb_pa_e_kernel(tc, x, h, Wv_words, Wv_scales, W1_words, W1_sc
         def load_wv_planes(s):
             load_scale_planes(nc, wv_planes_loaded[s], Wv_scales[PLANES * s : PLANES * (s + 1)])
 
+        def load_rows(rows, source, pair):
+            for r in range(PAIR * pair, PAIR * (pair + 1)):
+                nc.sync.dma_start(out=rows[r][:], in_=source[r])
+
+        load_rows(h_rows, h, 0)
         load_wv_planes(0)
-        for r in range(TOKEN_TILES):
-            nc.sync.dma_start(out=h_rows[r][:], in_=h[r])
         load_wv(0, 0)
+        load_rows(h_rows, h, 1)
         load_wv(0, 1)
-        for r in range(TOKEN_TILES):
-            nc.sync.dma_start(out=x_rows[r][:], in_=x[r])
+        load_rows(x_rows, x, 0)
+        load_rows(x_rows, x, 1)
         load_wv(1, 0)
+        load_wv(1, 1)
         for e in range(SUBNETS):
             load_scale_planes(nc, w1_planes[e], W1_scales[w1_groups(e)])
         load_w1(0)
-        load_wv(1, 1)
-        load_w1(1)
         load_wv_planes(1)
         load_wv(2, 0)
         load_wv(2, 1)
-        load_w1(2)
+        load_w1(1)
         load_wv(3, 0)
         load_wv(3, 1)
+        load_w1(2)
         load_w1(3)
 
         h_codes = keep.tile([P, TOKEN_TILES, PASSES, P], U32, name="h_codes", align_bytes=64)
         h_scales = keep.tile([P, TOKEN_TILES, PASSES, P], U8, name="h_scales", align_bytes=64)
         x_codes = keep.tile([P, TOKEN_TILES, PASSES, P], U32, name="x_codes", align_bytes=64)
         x_scales = keep.tile([P, TOKEN_TILES, PASSES, P], U8, name="x_scales", align_bytes=64)
-        x_sorted = [keep.tile([P, D], BF16, name="x_sorted%d" % r) for r in range(TOKEN_TILES)]
 
         def words_in_feature_order(rows):
             return rows[:].bitcast(F32).rearrange("r (c p u) -> r c u p", c=PASSES, u=2)
 
-        def words_sorted(rows):
-            return rows[:].bitcast(F32).rearrange("r (c u p) -> r c u p", c=PASSES, u=2)
+        def transpose_tiles(rows, pair, vector_helps):
+            tiles = rows[PAIR * pair : PAIR * (pair + 1)]
+            return transpose_pair(
+                nc, banks, work, identity, [words_in_feature_order(t) for t in tiles], vector_helps
+            )
 
-        def quantise_tiles(word_views, codes, scales, vector_helps):
-            for pair in range(PAIRS):
-                tiles = slice(PAIR * pair, PAIR * (pair + 1))
-                transpose_and_quantise(
-                    nc, banks, work, identity, word_views[tiles],
-                    codes[:, tiles].rearrange("p r c t -> p (r c t)"),
-                    scales[:, tiles].rearrange("p r c t -> p (r c t)"),
-                    vector_helps,
-                )
-
-        def sort_x():
-            for r in range(TOKEN_TILES):
-                nc.vector.tensor_copy(out=words_sorted(x_sorted[r]), in_=words_in_feature_order(x_rows[r]))
+        def quantise_tiles(grouped, pair, codes, scales):
+            tiles = slice(PAIR * pair, PAIR * (pair + 1))
+            nc.vector.quantize_mx(
+                out=codes[:, tiles].rearrange("p r c t -> p (r c t)").bitcast(FP8X4),
+                scales=scales[:, tiles].rearrange("p r c t -> p (r c t)"),
+                in_=grouped[:].rearrange("p j k -> p (j k)"),
+            )
 
         def sort_wv_planes(s, a):
             columns = slice(a * K_PASS, (a + 1) * K_PASS)
@@ -209,13 +206,13 @@ def tile_distributedb_pa_e_kernel(tc, x, h, Wv_words, Wv_scales, W1_words, W1_sc
                     stop=(c == PASSES - 1),
                 )
 
-        def round_views(e, a, r):
+        def round_views(j, e, a, r):
             unit = TOKEN_TILES * e + r
             if a == 0:
                 grouped = work.tile([P, PASSES, P, PACK], BF16, tag="views_grouped", align_bytes=64, bufs=8)
                 views_grouped[unit] = grouped
             four_apart = views_banks[(e, a, r)][:].rearrange("p t n -> p n t")
-            if r == VECTOR_BANK:
+            if j % 4 == VECTOR_BANK:
                 nc.vector.tensor_copy(out=views_grouped[unit][:, a, :, :], in_=four_apart)
             else:
                 nc.scalar.copy(out=views_grouped[unit][:, a, :, :], in_=four_apart)
@@ -251,45 +248,51 @@ def tile_distributedb_pa_e_kernel(tc, x, h, Wv_words, Wv_scales, W1_words, W1_sc
             nc.sync.dma_start(out=out[e, r], in_=mid[:])
 
         def split(j):
-            phase, r = divmod(j, TOKEN_TILES)
-            e, a = divmod(phase, PASSES)
-            return e, a, r
+            e, rest = divmod(j, 2 * TOKEN_TILES)
+            pair, rest = divmod(rest, 2 * PAIR)
+            a, second = divmod(rest, PAIR)
+            return e, a, PAIR * pair + second
 
         stage2_after = {}
         for unit in range(UNITS):
             e, r = divmod(unit, TOKEN_TILES)
-            stage2_after.setdefault(min(2 * TOKEN_TILES * e + STAGE2_DELAY + 2 * r, STEPS), []).append(unit)
+            step = max(2 * TOKEN_TILES * e + 2 * r + STAGE2_DELAY, X_READY + unit)
+            stage2_after.setdefault(min(step, STEPS), []).append(unit)
 
+        h_grouped = transpose_tiles(h_rows, 0, True)
         sort_wv_planes(0, 0)
-        quantise_tiles([words_in_feature_order(rows) for rows in h_rows], h_codes, h_scales, False)
+        quantise_tiles(h_grouped, 0, h_codes, h_scales)
         for j in range(STEPS + 1):
             if j == 0:
-                for r in range(TOKEN_TILES):
+                for r in range(PAIR):
                     open_bank(0, 0, r)
                 for t in range(PACK):
                     sort_wv(0, 0, t, t + 1)
-                    for r in range(TOKEN_TILES):
+                    for r in range(PAIR):
                         stage1_passes(0, 0, r, t)
+                h_grouped = transpose_tiles(h_rows, 1, False)
                 sort_wv_planes(0, 1)
+                sort_wv(0, 1, 0, PACK)
+                quantise_tiles(h_grouped, 1, h_codes, h_scales)
             if j < STEPS:
                 e, a, r = split(j)
-                if j >= TOKEN_TILES:
+                if j >= PAIR:
                     open_bank(e, a, r)
                     for t in range(PACK):
                         stage1_passes(e, a, r, t)
-                round_views(e, a, r)
+                round_views(j, e, a, r)
             if j >= 1:
                 e_done, a_done, r_done = split(j - 1)
                 if a_done == PASSES - 1:
                     quantise_views(TOKEN_TILES * e_done + r_done)
-            if j == TOKEN_TILES:
-                sort_x()
-            if j % TOKEN_TILES == 1 and j + 3 < STEPS:
-                e_next, a_next, r_next = split(j + 3)
-                sort_wv(e_next, a_next, 0, PACK)
+            e_now, rest = divmod(j, 2 * TOKEN_TILES)
+            if e_now + 1 < SUBNETS and rest in (5, 7):
+                sort_wv(e_now + 1, (rest - 5) // 2, 0, PACK)
             if j == 12 or j == 13:
                 sort_wv_planes(1, j - 12)
             if j == 2 * TOKEN_TILES - 1:
-                quantise_tiles([words_sorted(rows) for rows in x_sorted], x_codes, x_scales, True)
+                for pair in range(PAIRS):
+                    x_grouped = transpose_tiles(x_rows, pair, True)
+                    quantise_tiles(x_grouped, pair, x_codes, x_scales)
             for unit in stage2_after.get(j, []):
                 stage2(unit)

@@ -129,8 +129,8 @@ def tile_distributedb_pa_e_kernel(tc, x, h, Wv_words, Wv_scales, W1_words, W1_sc
 
         load_rows(h_rows, h, 0)
         load_wv_planes(0)
-        load_wv(0, 0)
         load_rows(h_rows, h, 1)
+        load_wv(0, 0)
         load_wv(0, 1)
         load_rows(x_rows, x, 0)
         load_rows(x_rows, x, 1)
@@ -212,7 +212,7 @@ def tile_distributedb_pa_e_kernel(tc, x, h, Wv_words, Wv_scales, W1_words, W1_sc
                 grouped = work.tile([P, PASSES, P, PACK], BF16, tag="views_grouped", align_bytes=64, bufs=8)
                 views_grouped[unit] = grouped
             four_apart = views_banks[(e, a, r)][:].rearrange("p t n -> p n t")
-            if j % 4 == VECTOR_BANK:
+            if e > 0 and j % 4 == VECTOR_BANK:
                 nc.vector.tensor_copy(out=views_grouped[unit][:, a, :, :], in_=four_apart)
             else:
                 nc.scalar.copy(out=views_grouped[unit][:, a, :, :], in_=four_apart)
@@ -249,6 +249,9 @@ def tile_distributedb_pa_e_kernel(tc, x, h, Wv_words, Wv_scales, W1_words, W1_sc
 
         def split(j):
             e, rest = divmod(j, 2 * TOKEN_TILES)
+            if e == 0:
+                a, r = divmod(rest, TOKEN_TILES)
+                return e, a, r
             pair, rest = divmod(rest, 2 * PAIR)
             a, second = divmod(rest, PAIR)
             return e, a, PAIR * pair + second
@@ -259,9 +262,10 @@ def tile_distributedb_pa_e_kernel(tc, x, h, Wv_words, Wv_scales, W1_words, W1_sc
             step = max(2 * TOKEN_TILES * e + 2 * r + STAGE2_DELAY, X_READY + unit)
             stage2_after.setdefault(min(step, STEPS), []).append(unit)
 
-        h_grouped = transpose_tiles(h_rows, 0, True)
+        h_grouped = [transpose_tiles(h_rows, pair, False) for pair in range(PAIRS)]
         sort_wv_planes(0, 0)
-        quantise_tiles(h_grouped, 0, h_codes, h_scales)
+        sort_wv_planes(0, 1)
+        quantise_tiles(h_grouped[0], 0, h_codes, h_scales)
         for j in range(STEPS + 1):
             if j == 0:
                 for r in range(PAIR):
@@ -270,10 +274,8 @@ def tile_distributedb_pa_e_kernel(tc, x, h, Wv_words, Wv_scales, W1_words, W1_sc
                     sort_wv(0, 0, t, t + 1)
                     for r in range(PAIR):
                         stage1_passes(0, 0, r, t)
-                h_grouped = transpose_tiles(h_rows, 1, False)
-                sort_wv_planes(0, 1)
+                quantise_tiles(h_grouped[1], 1, h_codes, h_scales)
                 sort_wv(0, 1, 0, PACK)
-                quantise_tiles(h_grouped, 1, h_codes, h_scales)
             if j < STEPS:
                 e, a, r = split(j)
                 if j >= PAIR:

@@ -243,7 +243,7 @@ def tile_distributedb_pa_e_kernel(tc, x, h, Wv_words, Wv_scales, W1_words, W1_sc
                     start=(g == 0),
                     stop=(g == 2 * PASSES - 1),
                 )
-            mid = work.tile([P, SD], F32, tag="mid")
+            mid = work.tile([P, SD], F32, tag="mid", bufs=UNITS)
             nc.scalar.activation(out=mid[:], in_=acc[:], func=SILU)
             nc.sync.dma_start(out=out[e, r], in_=mid[:])
 

@@ -25,7 +25,7 @@ PAIRS = TOKEN_TILES // PAIR
 PLANES = 4
 STEPS = SUBNETS * PASSES * TOKEN_TILES
 STAGE2_DELAY = 5
-X_READY = 10
+X_READY = 12
 VECTOR_BANK = 0
 
 FLOPS = 2 * TOKEN_TILES * P * SUBNETS * (D * D + 2 * D * SD)

@@ -20,6 +20,7 @@ UNITS = SUBNETS * TOKEN_TILES
 D = 1024
 PASSES = D // K_PASS
 SD = 256
+W1_GROUPS = SUBNETS * 2 * PASSES
 PAIR = 2
 PAIRS = TOKEN_TILES // PAIR
 PLANES = 4
@@ -73,11 +74,10 @@ def tile_distributedb_pa_e_kernel(tc, x, h, Wv_words, Wv_scales, W1_words, W1_sc
             keep.tile([P, D], U8, name="wv_planes%d" % s, align_bytes=64)
             for s in range(SUBNETS * PASSES // PLANES)
         ]
-        w1_planes = [
-            keep.tile([P, SD], U8, name="w1_planes%d" % e, align_bytes=64) for e in range(SUBNETS)
-        ]
-        for planes in wv_planes_loaded + w1_planes:
+        w1_planes = keep.tile([P, W1_GROUPS, SD], U8, name="w1_planes", align_bytes=64)
+        for planes in wv_planes_loaded:
             nc.vector.memset(planes[:].bitcast(I32), 0)
+        nc.vector.memset(w1_planes[:].rearrange("p g n -> p (g n)").bitcast(I32), 0)
         identity = keep.tile([P, P], F32, name="identity")
         make_identity(nc, identity[:])
         zero = keep.tile([P, 1], F32, name="zero")
@@ -120,6 +120,13 @@ def tile_distributedb_pa_e_kernel(tc, x, h, Wv_words, Wv_scales, W1_words, W1_sc
                 in_=W1_words[w1_groups(e)].rearrange("g p n t -> p g (n t)").bitcast(I32),
             )
 
+        def load_w1_planes():
+            for quadrant in range(4):
+                nc.sync.dma_start(
+                    out=w1_planes[32 * quadrant : 32 * quadrant + 4, :, :].rearrange("p g n -> p (g n)").bitcast(I32).rearrange("p (g n) -> p g n", g=W1_GROUPS),
+                    in_=W1_scales[:, 4 * quadrant : 4 * quadrant + 4, :].rearrange("g q n -> q g n").bitcast(I32),
+                )
+
         def load_wv_planes(s):
             load_scale_planes(nc, wv_planes_loaded[s], Wv_scales[PLANES * s : PLANES * (s + 1)])
 
@@ -136,10 +143,9 @@ def tile_distributedb_pa_e_kernel(tc, x, h, Wv_words, Wv_scales, W1_words, W1_sc
         load_rows(x_rows, x, 1)
         load_wv(1, 0)
         load_wv(1, 1)
-        for e in range(SUBNETS):
-            load_scale_planes(nc, w1_planes[e], W1_scales[w1_groups(e)])
-        load_w1(0)
+        load_w1_planes()
         load_wv_planes(1)
+        load_w1(0)
         load_wv(2, 0)
         load_wv(2, 1)
         load_w1(1)
@@ -239,7 +245,7 @@ def tile_distributedb_pa_e_kernel(tc, x, h, Wv_words, Wv_scales, W1_words, W1_sc
                     lhsT=operands[g][0].bitcast(FP8X4),
                     lhsT_scale=operands[g][1],
                     rhs=w1_words[e][:, g, :].bitcast(FP8X4),
-                    rhs_scale=w1_planes[e][4 * g : P, :],
+                    rhs_scale=w1_planes[:, 2 * PASSES * e + g, :],
                     start=(g == 0),
                     stop=(g == 2 * PASSES - 1),
                 )

@@ -26,6 +26,7 @@ PAIRS = TOKEN_TILES // PAIR
 PLANES = 4
 STEPS = SUBNETS * PASSES * TOKEN_TILES
 STAGE2_DELAY = 5
+X_STEPS = [7, 9]
 X_READY = 12
 VECTOR_BANK = 0
 
@@ -183,7 +184,14 @@ def tile_distributedb_pa_e_kernel(tc, x, h, Wv_words, Wv_scales, W1_words, W1_sc
                 in_=wv_planes_loaded[s][:, columns].rearrange("p (m t) -> p t m", t=PACK),
             )
 
-        def sort_wv(e, a, t_from, t_to):
+        def sort_wv(e, a):
+            for c in range(PASSES):
+                nc.vector.tensor_copy(
+                    out=wv_sorted[e][a][:, c, :].bitcast(I32).rearrange("p (t m i) -> p m t i", t=PACK, i=4),
+                    in_=wv_loaded[e][a][:, c, :].bitcast(I32).rearrange("p (m i t) -> p m t i", t=PACK, i=4),
+                )
+
+        def sort_first_wv(e, a, t_from, t_to):
             nc.vector.tensor_copy(
                 out=wv_sorted[e][a][:].bitcast(I32).rearrange("p c (t m) -> p c t m", t=PACK)[:, :, t_from:t_to, :],
                 in_=wv_loaded[e][a][:].bitcast(I32).rearrange("p c (m t) -> p c t m", t=PACK)[:, :, t_from:t_to, :],
@@ -277,11 +285,11 @@ def tile_distributedb_pa_e_kernel(tc, x, h, Wv_words, Wv_scales, W1_words, W1_sc
                 for r in range(PAIR):
                     open_bank(0, 0, r)
                 for t in range(PACK):
-                    sort_wv(0, 0, t, t + 1)
+                    sort_first_wv(0, 0, t, t + 1)
                     for r in range(PAIR):
                         stage1_passes(0, 0, r, t)
                 quantise_tiles(h_grouped[1], 1, h_codes, h_scales)
-                sort_wv(0, 1, 0, PACK)
+                sort_wv(0, 1)
             if j < STEPS:
                 e, a, r = split(j)
                 if j >= PAIR:
@@ -295,12 +303,12 @@ def tile_distributedb_pa_e_kernel(tc, x, h, Wv_words, Wv_scales, W1_words, W1_sc
                     quantise_views(TOKEN_TILES * e_done + r_done)
             e_now, rest = divmod(j, 2 * TOKEN_TILES)
             if e_now + 1 < SUBNETS and rest in (5, 7):
-                sort_wv(e_now + 1, (rest - 5) // 2, 0, PACK)
+                sort_wv(e_now + 1, (rest - 5) // 2)
             if j == 12 or j == 13:
                 sort_wv_planes(1, j - 12)
-            if j == 2 * TOKEN_TILES - 1:
-                for pair in range(PAIRS):
-                    x_grouped = transpose_tiles(x_rows, pair, True)
-                    quantise_tiles(x_grouped, pair, x_codes, x_scales)
+            if j in X_STEPS:
+                pair = X_STEPS.index(j)
+                x_grouped = transpose_tiles(x_rows, pair, True)
+                quantise_tiles(x_grouped, pair, x_codes, x_scales)
             for unit in stage2_after.get(j, []):
                 stage2(unit)

@@ -26,6 +26,7 @@ PAIRS = TOKEN_TILES // PAIR
 PLANES = 4
 STEPS = SUBNETS * PASSES * TOKEN_TILES
 STAGE2_DELAY = 5
+X_SORTS = [4, 6]
 X_STEPS = [7, 9]
 X_READY = 12
 VECTOR_BANK = 0
@@ -160,14 +161,15 @@ def tile_distributedb_pa_e_kernel(tc, x, h, Wv_words, Wv_scales, W1_words, W1_sc
         x_codes = keep.tile([P, TOKEN_TILES, PASSES, P], U32, name="x_codes", align_bytes=64)
         x_scales = keep.tile([P, TOKEN_TILES, PASSES, P], U8, name="x_scales", align_bytes=64)
 
-        def words_in_feature_order(rows):
-            return rows[:].bitcast(F32).rearrange("r (c p u) -> r c u p", c=PASSES, u=2)
-
-        def transpose_tiles(rows, pair, vector_helps):
-            tiles = rows[PAIR * pair : PAIR * (pair + 1)]
-            return transpose_pair(
-                nc, banks, work, identity, [words_in_feature_order(t) for t in tiles], vector_helps
+        def sort_words(rows):
+            in_order = work.tile([P, PASSES, 2, P], F32, tag="in_order", bufs=8)
+            nc.vector.tensor_copy(
+                out=in_order[:], in_=rows[:].bitcast(F32).rearrange("r (c p u) -> r c u p", c=PASSES, u=2)
             )
+            return in_order
+
+        def transpose_tiles(word_tiles, vector_helps):
+            return transpose_pair(nc, banks, work, identity, [t[:] for t in word_tiles], vector_helps)
 
         def quantise_tiles(grouped, pair, codes, scales):
             tiles = slice(PAIR * pair, PAIR * (pair + 1))
@@ -276,10 +278,14 @@ def tile_distributedb_pa_e_kernel(tc, x, h, Wv_words, Wv_scales, W1_words, W1_sc
             step = max(2 * TOKEN_TILES * e + 2 * r + STAGE2_DELAY, X_READY + unit)
             stage2_after.setdefault(min(step, STEPS), []).append(unit)
 
-        h_grouped = [transpose_tiles(h_rows, pair, False) for pair in range(PAIRS)]
+        h_words = [sort_words(rows) for rows in h_rows[:3]]
         sort_wv_planes(0, 0)
-        sort_wv_planes(0, 1)
+        h_words.append(sort_words(h_rows[3]))
+        h_grouped = [
+            transpose_tiles(h_words[PAIR * pair : PAIR * (pair + 1)], False) for pair in range(PAIRS)
+        ]
         quantise_tiles(h_grouped[0], 0, h_codes, h_scales)
+        x_words = []
         for j in range(STEPS + 1):
             if j == 0:
                 for r in range(PAIR):
@@ -289,6 +295,7 @@ def tile_distributedb_pa_e_kernel(tc, x, h, Wv_words, Wv_scales, W1_words, W1_sc
                     for r in range(PAIR):
                         stage1_passes(0, 0, r, t)
                 quantise_tiles(h_grouped[1], 1, h_codes, h_scales)
+                sort_wv_planes(0, 1)
                 sort_wv(0, 1)
             if j < STEPS:
                 e, a, r = split(j)
@@ -301,6 +308,9 @@ def tile_distributedb_pa_e_kernel(tc, x, h, Wv_words, Wv_scales, W1_words, W1_sc
                 e_done, a_done, r_done = split(j - 1)
                 if a_done == PASSES - 1:
                     quantise_views(TOKEN_TILES * e_done + r_done)
+            if j in X_SORTS:
+                for i in range(PAIR):
+                    x_words.append(sort_words(x_rows[len(x_words)]))
             e_now, rest = divmod(j, 2 * TOKEN_TILES)
             if e_now + 1 < SUBNETS and rest in (5, 7):
                 sort_wv(e_now + 1, (rest - 5) // 2)
@@ -308,7 +318,7 @@ def tile_distributedb_pa_e_kernel(tc, x, h, Wv_words, Wv_scales, W1_words, W1_sc
                 sort_wv_planes(1, j - 12)
             if j in X_STEPS:
                 pair = X_STEPS.index(j)
-                x_grouped = transpose_tiles(x_rows, pair, True)
+                x_grouped = transpose_tiles(x_words[PAIR * pair : PAIR * (pair + 1)], True)
                 quantise_tiles(x_grouped, pair, x_codes, x_scales)
             for unit in stage2_after.get(j, []):
                 stage2(unit)

from contextlib import ExitStack

import concourse.mybir as mybir
from concourse.masks import make_identity

F32 = mybir.dt.float32
BF16 = mybir.dt.bfloat16
I32 = mybir.dt.int32
U32 = mybir.dt.uint32
U8 = mybir.dt.uint8
FP8X4 = mybir.dt.float8_e4m3fn_x4
SILU = mybir.ActivationFunctionType.Silu

P = 128
PACK = 4
K_PASS = P * PACK
SUBNETS = 4
TOKEN_TILES = 4
UNITS = SUBNETS * TOKEN_TILES
D = 1024
PASSES = D // K_PASS
SD = 256
W1_GROUPS = SUBNETS * 2 * PASSES
PAIR = 2
PAIRS = TOKEN_TILES // PAIR
PLANES = 4
STEPS = SUBNETS * PASSES * TOKEN_TILES
STAGE2_DELAY = 5
X_SORTS = [4, 6]
X_STEPS = [7, 9]
X_READY = 12
VECTOR_BANK = 0

FLOPS = 2 * TOKEN_TILES * P * SUBNETS * (D * D + 2 * D * SD)


def load_scale_planes(nc, planes, scale_rows):
    for quadrant in range(4):
        nc.sync.dma_start(
            out=planes[32 * quadrant : 32 * quadrant + 4 * PLANES, :].bitcast(I32),
            in_=scale_rows[:, 4 * quadrant : 4 * quadrant + 4, :].bitcast(I32),
        )


def transpose_pair(nc, banks, work, identity, word_views, vector_helps):
    grouped = work.tile([P, PAIR, D], BF16, tag="grouped", align_bytes=64)
    for j in range(PAIR):
        flipped = banks.tile([P, PASSES, 2, P], F32, tag="bank")
        for c in range(PASSES):
            for u in range(2):
                nc.tensor.transpose(
                    out=flipped[:, c, u, :], in_=word_views[j][:, c, u, :], identity=identity[:]
                )
        side_by_side = grouped[:, j, :].bitcast(F32).rearrange("p (c r u) -> p c r u", c=PASSES, u=2)
        planes_apart = flipped[:].rearrange("p c u r -> p c r u")
        if j == 0 and vector_helps:
            nc.vector.tensor_copy(out=side_by_side, in_=planes_apart)
        else:
            nc.scalar.copy(out=side_by_side, in_=planes_apart)
    return grouped


def tile_distributedb_pa_e_kernel(tc, x, h, Wv_words, Wv_scales, W1_words, W1_scales, out):
    nc = tc.nc
    with ExitStack() as ctx:
        keep = ctx.enter_context(tc.tile_pool(name="keep", bufs=1))
        work = ctx.enter_context(tc.tile_pool(name="work", bufs=4))
        banks = ctx.enter_context(tc.psum_pool(name="banks", bufs=8))
        ctx.enter_context(tc.manual_schedule())

        wv_planes_loaded = [
            keep.tile([P, D], U8, name="wv_planes_loaded%d" % s, align_bytes=64)
            for s in range(SUBNETS * PASSES // PLANES)
        ]
        wv_planes = [
            keep.tile([P, D], U8, name="wv_planes%d" % s, align_bytes=64)
            for s in range(SUBNETS * PASSES // PLANES)
        ]
        w1_planes = keep.tile([P, W1_GROUPS, SD], U8, name="w1_planes", align_bytes=64)
        for planes in wv_planes_loaded:
            nc.vector.memset(planes[:].bitcast(I32), 0)
        nc.vector.memset(w1_planes[:].rearrange("p g n -> p (g n)").bitcast(I32), 0)
        identity = keep.tile([P, P], F32, name="identity")
        make_identity(nc, identity[:])
        zero = keep.tile([P, 1], F32, name="zero")
        nc.vector.memset(zero[:], 0.0)
        table_warm = keep.tile([P, 1], F32, name="table_warm")
        nc.scalar.activation(out=table_warm[:], in_=zero[:], func=SILU)

        h_rows = [keep.tile([P, D], BF16, name="h_rows%d" % r) for r in range(TOKEN_TILES)]
        x_rows = [keep.tile([P, D], BF16, name="x_rows%d" % r) for r in range(TOKEN_TILES)]
        wv_loaded = [
            [keep.tile([P, PASSES, K_PASS], U32, name="wv_loaded%d_%d" % (e, a), align_bytes=64)
             for a in range(PASSES)]
            for e in range(SUBNETS)
        ]
        wv_sorted = [
            [keep.tile([P, PASSES, K_PASS], U32, name="wv_sorted%d_%d" % (e, a), align_bytes=64)
             for a in range(PASSES)]
            for e in range(SUBNETS)
        ]
        w1_words = [
            keep.tile([P, 2 * PASSES, SD], U32, name="w1_words%d" % e, align_bytes=64)
            for e in range(SUBNETS)
        ]

        def load_wv(e, a):
            columns = slice(a * K_PASS, (a + 1) * K_PASS)
            nc.sync.dma_start(
                out=wv_loaded[e][a][:].bitcast(I32),
                in_=Wv_words[PASSES * e : PASSES * (e + 1), :, columns, :]
                .rearrange("c p n t -> p c (n t)")
                .bitcast(I32),
            )

        def w1_groups(e):
            return slice(2 * PASSES * e, 2 * PASSES * (e + 1))

        def load_w1(e):
            nc.sync.dma_start(
                out=w1_words[e][:].bitcast(I32),
                in_=W1_words[w1_groups(e)].rearrange("g p n t -> p g (n t)").bitcast(I32),
            )

        def load_w1_planes():
            for quadrant in range(4):
                nc.sync.dma_start(
                    out=w1_planes[32 * quadrant : 32 * quadrant + 4, :, :].rearrange("p g n -> p (g n)").bitcast(I32).rearrange("p (g n) -> p g n", g=W1_GROUPS),
                    in_=W1_scales[:, 4 * quadrant : 4 * quadrant + 4, :].rearrange("g q n -> q g n").bitcast(I32),
                )

        def load_wv_planes(s):
            load_scale_planes(nc, wv_planes_loaded[s], Wv_scales[PLANES * s : PLANES * (s + 1)])

        def load_rows(rows, source, pair):
            for r in range(PAIR * pair, PAIR * (pair + 1)):
                nc.sync.dma_start(out=rows[r][:], in_=source[r])

        load_rows(h_rows, h, 0)
        load_wv_planes(0)
        load_rows(h_rows, h, 1)
        load_wv(0, 0)
        load_wv(0, 1)
        load_rows(x_rows, x, 0)
        load_rows(x_rows, x, 1)
        load_wv(1, 0)
        load_wv(1, 1)
        load_w1_planes()
        load_wv_planes(1)
        load_w1(0)
        load_wv(2, 0)
        load_wv(2, 1)
        load_w1(1)
        load_wv(3, 0)
        load_wv(3, 1)
        load_w1(2)
        load_w1(3)

        h_codes = keep.tile([P, TOKEN_TILES, PASSES, P], U32, name="h_codes", align_bytes=64)
        h_scales = keep.tile([P, TOKEN_TILES, PASSES, P], U8, name="h_scales", align_bytes=64)
        x_codes = keep.tile([P, TOKEN_TILES, PASSES, P], U32, name="x_codes", align_bytes=64)
        x_scales = keep.tile([P, TOKEN_TILES, PASSES, P], U8, name="x_scales", align_bytes=64)

        def sort_words(rows):
            in_order = work.tile([P, PASSES, 2, P], F32, tag="in_order", bufs=8)
            nc.vector.tensor_copy(
                out=in_order[:], in_=rows[:].bitcast(F32).rearrange("r (c p u) -> r c u p", c=PASSES, u=2)
            )
            return in_order

        def transpose_tiles(word_tiles, vector_helps):
            return transpose_pair(nc, banks, work, identity, [t[:] for t in word_tiles], vector_helps)

        def quantise_tiles(grouped, pair, codes, scales):
            tiles = slice(PAIR * pair, PAIR * (pair + 1))
            nc.vector.quantize_mx(
                out=codes[:, tiles].rearrange("p r c t -> p (r c t)").bitcast(FP8X4),
                scales=scales[:, tiles].rearrange("p r c t -> p (r c t)"),
                in_=grouped[:].rearrange("p j k -> p (j k)"),
            )

        def sort_wv_planes(s, a):
            columns = slice(a * K_PASS, (a + 1) * K_PASS)
            nc.vector.tensor_copy(
                out=wv_planes[s][:, columns].rearrange("p (t m) -> p t m", t=PACK),
                in_=wv_planes_loaded[s][:, columns].rearrange("p (m t) -> p t m", t=PACK),
            )

        def sort_wv(e, a):
            for c in range(PASSES):
                nc.vector.tensor_copy(
                    out=wv_sorted[e][a][:, c, :].bitcast(I32).rearrange("p (t m i) -> p m t i", t=PACK, i=4),
                    in_=wv_loaded[e][a][:, c, :].bitcast(I32).rearrange("p (m i t) -> p m t i", t=PACK, i=4),
                )

        def sort_first_wv(e, a, t_from, t_to):
            nc.vector.tensor_copy(
                out=wv_sorted[e][a][:].bitcast(I32).rearrange("p c (t m) -> p c t m", t=PACK)[:, :, t_from:t_to, :],
                in_=wv_loaded[e][a][:].bitcast(I32).rearrange("p c (m t) -> p c t m", t=PACK)[:, :, t_from:t_to, :],
            )

        views_banks = {}
        views_grouped = {}
        views_mx = {}

        def open_bank(e, a, r):
            acc = banks.tile([P, PACK, P], F32, tag="bank")
            views_banks[(e, a, r)] = acc

        def stage1_passes(e, a, r, t):
            for c in range(PASSES):
                group = PASSES * e + c
                nc.tensor.matmul_mx(
                    out=views_banks[(e, a, r)][:, t, :],
                    lhsT=wv_sorted[e][a][:, c, t * P : (t + 1) * P].bitcast(FP8X4),
                    lhsT_scale=wv_planes[group // PLANES][
                        4 * (group % PLANES) : P, a * K_PASS + t * P : a * K_PASS + (t + 1) * P
                    ],
                    rhs=h_codes[:, r, c, :].bitcast(FP8X4),
                    rhs_scale=h_scales[:, r, c, :],
                    start=(c == 0),
                    stop=(c == PASSES - 1),
                )

        def round_views(j, e, a, r):
            unit = TOKEN_TILES * e + r
            if a == 0:
                grouped = work.tile([P, PASSES, P, PACK], BF16, tag="views_grouped", align_bytes=64, bufs=8)
                views_grouped[unit] = grouped
            four_apart = views_banks[(e, a, r)][:].rearrange("p t n -> p n t")
            if e > 0 and j % 4 == VECTOR_BANK:
                nc.vector.tensor_copy(out=views_grouped[unit][:, a, :, :], in_=four_apart)
            else:
                nc.scalar.copy(out=views_grouped[unit][:, a, :, :], in_=four_apart)

        def quantise_views(unit):
            codes = work.tile([P, PASSES, P], U32, tag="views_codes", align_bytes=64, bufs=8)
            scales = work.tile([P, PASSES, P], U8, tag="views_scales", align_bytes=64, bufs=8)
            views_mx[unit] = (codes, scales)
            nc.vector.quantize_mx(
                out=codes[:].rearrange("p a n -> p (a n)").bitcast(FP8X4),
                scales=scales[:].rearrange("p a n -> p (a n)"),
                in_=views_grouped[unit][:].rearrange("p a n t -> p (a n t)"),
            )

        def stage2(unit):
            e, r = divmod(unit, TOKEN_TILES)
            codes, scales = views_mx[unit]
            operands = [(x_codes[:, r, c, :], x_scales[:, r, c, :]) for c in range(PASSES)]
            operands += [(codes[:, a, :], scales[:, a, :]) for a in range(PASSES)]
            acc = banks.tile([P, SD], F32, tag="bank")
            for g in range(2 * PASSES):
                nc.tensor.matmul_mx(
                    out=acc[:],
                    lhsT=operands[g][0].bitcast(FP8X4),
                    lhsT_scale=operands[g][1],
                    rhs=w1_words[e][:, g, :].bitcast(FP8X4),
                    rhs_scale=w1_planes[:, 2 * PASSES * e + g, :],
                    start=(g == 0),
                    stop=(g == 2 * PASSES - 1),
                )
            mid = work.tile([P, SD], F32, tag="mid", bufs=UNITS)
            nc.scalar.activation(out=mid[:], in_=acc[:], func=SILU)
            nc.sync.dma_start(out=out[e, r], in_=mid[:])

        def split(j):
            e, rest = divmod(j, 2 * TOKEN_TILES)
            if e == 0:
                a, r = divmod(rest, TOKEN_TILES)
                return e, a, r
            pair, rest = divmod(rest, 2 * PAIR)
            a, second = divmod(rest, PAIR)
            return e, a, PAIR * pair + second

        stage2_after = {}
        for unit in range(UNITS):
            e, r = divmod(unit, TOKEN_TILES)
            step = max(2 * TOKEN_TILES * e + 2 * r + STAGE2_DELAY, X_READY + unit)
            stage2_after.setdefault(min(step, STEPS), []).append(unit)

        h_words = [sort_words(rows) for rows in h_rows[:3]]
        sort_wv_planes(0, 0)
        h_words.append(sort_words(h_rows[3]))
        h_grouped = [
            transpose_tiles(h_words[PAIR * pair : PAIR * (pair + 1)], False) for pair in range(PAIRS)
        ]
        quantise_tiles(h_grouped[0], 0, h_codes, h_scales)
        x_words = []
        for j in range(STEPS + 1):
            if j == 0:
                for r in range(PAIR):
                    open_bank(0, 0, r)
                for t in range(PACK):
                    sort_first_wv(0, 0, t, t + 1)
                    for r in range(PAIR):
                        stage1_passes(0, 0, r, t)
                quantise_tiles(h_grouped[1], 1, h_codes, h_scales)
                sort_wv_planes(0, 1)
                sort_wv(0, 1)
            if j < STEPS:
                e, a, r = split(j)
                if j >= PAIR:
                    open_bank(e, a, r)
                    for t in range(PACK):
                        stage1_passes(e, a, r, t)
                round_views(j, e, a, r)
            if j >= 1:
                e_done, a_done, r_done = split(j - 1)
                if a_done == PASSES - 1:
                    quantise_views(TOKEN_TILES * e_done + r_done)
            if j in X_SORTS:
                for i in range(PAIR):
                    x_words.append(sort_words(x_rows[len(x_words)]))
            e_now, rest = divmod(j, 2 * TOKEN_TILES)
            if e_now + 1 < SUBNETS and rest in (5, 7):
                sort_wv(e_now + 1, (rest - 5) // 2)
            if j == 12 or j == 13:
                sort_wv_planes(1, j - 12)
            if j in X_STEPS:
                pair = X_STEPS.index(j)
                x_grouped = transpose_tiles(x_words[PAIR * pair : PAIR * (pair + 1)], True)
                quantise_tiles(x_grouped, pair, x_codes, x_scales)
            for unit in stage2_after.get(j, []):
                stage2(unit)
